import numpy as np
import ml_dtypes


def mxq(x, axis, fmt="e4m3"):
    dtype, down = {"e4m3": (ml_dtypes.float8_e4m3fn, 7), "e5m2": (ml_dtypes.float8_e5m2, 14)}[fmt]
    v = np.moveaxis(np.asarray(x, np.float32).astype(ml_dtypes.bfloat16).astype(np.float64), axis, -1)
    blocks = v.reshape(v.shape[:-1] + (-1, 32))
    amax = np.abs(blocks).max(-1, keepdims=True)
    byte = np.maximum(np.where(amax > 0, np.frexp(amax)[1] - 1 + 127, 0) - down, 1)
    scale = np.exp2(byte - 127.0)
    codes = (blocks / scale).astype(np.float32).astype(dtype).astype(np.float64)
    return np.moveaxis((codes * scale).reshape(v.shape), -1, axis)


WIDE = False


def mx_kscale(k):
    if not WIDE:
        return np.ones(k)
    levels = np.array([10, -10, 5, -5, 0])
    a = np.random.permutation(np.resize(levels, k // 512 * 4)).reshape(k // 512, 4)
    idx = np.arange(k)
    return np.exp2(a[idx // 512, idx % 128 // 32])


BF16 = ml_dtypes.bfloat16


def bf(x):
    return np.asarray(x, np.float32).astype(BF16)


def f64(x):
    return np.asarray(x).astype(np.float64)


N, D, C = 2048, 512, 1024


def gaussian_kernel(inputs, centers, gamma):
    x2 = np.sum(inputs * inputs, axis=-1, keepdims=True)
    c2 = np.sum(centers * centers, axis=-1)
    xc = mxq(inputs, 1, "e4m3") @ mxq(centers, 1, "e4m3").T
    sq_dist = np.maximum(x2 + c2[None, :] - 2.0 * xc, 0.0)
    return np.exp(-gamma * sq_dist)


def setup_inputs():
    t = mx_kscale(C)
    gamma = bf((1.0 + 0.1 * np.random.standard_normal(1)) / D)
    g = np.random.standard_normal((C, D))
    shift = np.log(t.max() / t) / f64(gamma)[0]
    centers = g * np.sqrt(1.0 + shift / (g * g).sum(1))[:, None]
    return {"inputs": bf(np.random.standard_normal((N, D))), "centers": bf(centers), "gamma": gamma,
            "normalization": bf(np.random.standard_normal((C, C)) * 4.0 / np.sqrt(C) * (t.max() / t)[:, None])}


def reference(inputs, centers, gamma, normalization):
    inputs = f64(inputs)
    inputs = inputs.reshape(inputs.shape[0], -1)
    densities = gaussian_kernel(inputs, f64(centers), f64(gamma))
    return mxq(densities, 1, "e4m3") @ mxq(f64(normalization), 0, "e4m3")

@@ -1,0 +1,212 @@
+from contextlib import ExitStack
+
+import concourse.mybir as mybir
+from concourse.masks import make_identity
+
+F32 = mybir.dt.float32
+BF16 = mybir.dt.bfloat16
+U32 = mybir.dt.uint32
+U8 = mybir.dt.uint8
+FP8X4 = mybir.dt.float8_e4m3fn_x4
+ALU = mybir.AluOpType
+ACT = mybir.ActivationFunctionType
+
+N, D, C = 2048, 512, 1024
+P = 128
+FLOPS = 2 * N * D * C + 2 * N * C * C
+
+CHUNKS = 4
+TILES = 4
+
+
+def tile_nystroem_kernel(tc, inputs, centers, gamma, normalization, out):
+    nc = tc.nc
+    with ExitStack() as ctx:
+        keep = ctx.enter_context(tc.tile_pool(name="keep", bufs=1))
+        work2 = ctx.enter_context(tc.tile_pool(name="work2", bufs=2))
+        work3 = ctx.enter_context(tc.tile_pool(name="work3", bufs=3))
+        outp = ctx.enter_context(tc.tile_pool(name="outp", bufs=4))
+        ps_t = ctx.enter_context(tc.psum_pool(name="ps_t", bufs=2))
+        ps_1 = ctx.enter_context(tc.psum_pool(name="ps_1", bufs=3))
+        ps_2 = ctx.enter_context(tc.psum_pool(name="ps_2", bufs=3))
+
+        x_view = inputs.rearrange("(p i) d -> p i d", i=CHUNKS * TILES)
+        c_view = centers.rearrange("(g p t) d -> g p t d", g=2, t=4)
+        n_view = normalization.rearrange("(g p t) j -> g p t j", g=2, t=4)
+        o_view = out.rearrange("(p i) j -> p i j", i=CHUNKS * TILES)
+
+        ident = keep.tile([P, P], F32)
+        g_bf = keep.tile([P, 1], BF16)
+        g2 = keep.tile([P, 1], F32)
+        warm = keep.tile([P, 1], F32)
+        c_sb = keep.tile([P, 2, 4, D], BF16)
+        x_sb = keep.tile([P, CHUNKS * TILES, D], BF16)
+        n_raw = keep.tile([P, 2, 4, C], BF16)
+        c_codes = keep.tile([P, C], U32, align_bytes=64)
+        c_scales = keep.tile([P, C], U8, align_bytes=64)
+        x_codes = keep.tile([P, N], U32, align_bytes=64)
+        x_scales = keep.tile([P, N], U8, align_bytes=64)
+        n_codes = keep.tile([P, 2, C], U32, align_bytes=64)
+        n_scales = keep.tile([P, 2, C], U8, align_bytes=64)
+        x2col = keep.tile([P, CHUNKS * TILES], F32)
+        c2col = keep.tile([P, 8], F32)
+        c2h = keep.tile([P, 8], F32)
+        x2hb = keep.tile([P, CHUNKS, 512], F32)
+
+        nc.scalar.dma_start(out=g_bf[:], in_=gamma.partition_broadcast(P))
+        nc.sync.dma_start(out=c_sb[:, 0], in_=c_view[0])
+        nc.sync.dma_start(out=x_sb[:, 0:4, :], in_=x_view[:, 0:4, :])
+        nc.sync.dma_start(out=c_sb[:, 1], in_=c_view[1])
+        nc.sync.dma_start(out=x_sb[:, 4:8, :], in_=x_view[:, 4:8, :])
+        nc.sync.dma_start(out=n_raw[:, 0], in_=n_view[0])
+        nc.sync.dma_start(out=n_raw[:, 1], in_=n_view[1])
+        nc.sync.dma_start(out=x_sb[:, 8:12, :], in_=x_view[:, 8:12, :])
+        nc.sync.dma_start(out=x_sb[:, 12:16, :], in_=x_view[:, 12:16, :])
+
+        make_identity(nc, ident[:])
+        nc.vector.memset(warm[:], 0.0)
+        nc.scalar.activation(out=warm[:], in_=warm[:], func=ACT.Exp)
+        nc.vector.tensor_scalar_mul(out=g2[:], in0=g_bf[:], scalar1=2.0)
+
+        def transpose_rows(row_tiles, grouped):
+            words = grouped[:].bitcast(F32).rearrange("p (c u) -> p c u", u=2)
+            for b in range(2):
+                tp = ps_t.tile([P, 2, 256], F32, tag="tp")
+                for a in range(2):
+                    src = row_tiles[2 * b + a].bitcast(F32)
+                    for u in range(2):
+                        nc.tensor.transpose(
+                            tp[:, u, 128 * a : 128 * a + 128],
+                            src[:, 128 * u : 128 * u + 128],
+                            ident[:],
+                        )
+                nc.vector.tensor_copy(
+                    out=words[:, 256 * b : 256 * b + 256, :],
+                    in_=tp[:].rearrange("p u c -> p c u"),
+                )
+
+        def squares(row_tiles, col_tile, first):
+            for a in range(4):
+                junk = work2.tile([P, D], BF16, tag="junk")
+                nc.scalar.activation(
+                    out=junk[:],
+                    in_=row_tiles[a],
+                    func=ACT.Square,
+                    accum_out=col_tile[:, first + a : first + a + 1],
+                )
+
+        def prep_centers(g):
+            rows = [c_sb[:, g, t, :] for t in range(4)]
+            squares(rows, c2col, 4 * g)
+            nc.vector.tensor_scalar_mul(
+                out=c2h[:, 4 * g : 4 * g + 4], in0=c2col[:, 4 * g : 4 * g + 4], scalar1=0.5
+            )
+            gc = work2.tile([P, 2048], BF16, tag="gc", align_bytes=64)
+            transpose_rows(rows, gc)
+            nc.vector.quantize_mx(
+                out=c_codes[:, 512 * g : 512 * g + 512].bitcast(FP8X4),
+                scales=c_scales[:, 512 * g : 512 * g + 512],
+                in_=gc[:],
+            )
+
+        def prep_inputs(q):
+            rows = [x_sb[:, 4 * q + a, :] for a in range(4)]
+            squares(rows, x2col, 4 * q)
+            gx = work2.tile([P, 2048], BF16, tag="gx", align_bytes=64)
+            transpose_rows(rows, gx)
+            nc.vector.quantize_mx(
+                out=x_codes[:, 512 * q : 512 * q + 512].bitcast(FP8X4),
+                scales=x_scales[:, 512 * q : 512 * q + 512],
+                in_=gx[:],
+            )
+            rep = work2.tile([P, 4, P], F32, tag="rep")
+            nc.vector.tensor_scalar_mul(
+                out=rep[:],
+                in0=x2col[:, 4 * q : 4 * q + 4].unsqueeze(2).to_broadcast([P, 4, P]),
+                scalar1=0.5,
+            )
+            tpx = ps_t.tile([P, 4, P], F32, tag="tp")
+            for a in range(4):
+                nc.tensor.transpose(tpx[:, a, :], rep[:, a, :], ident[:])
+            nc.scalar.copy(out=x2hb[:, q, :], in_=tpx[:].rearrange("p a c -> p (a c)"))
+
+        def prep_norm(g):
+            ng = work2.tile([P, C, 4], BF16, tag="ng", align_bytes=64)
+            nc.vector.tensor_copy(out=ng[:], in_=n_raw[:, g].rearrange("p t j -> p j t"))
+            nc.vector.quantize_mx(
+                out=n_codes[:, g, :].bitcast(FP8X4),
+                scales=n_scales[:, g, :],
+                in_=ng[:].rearrange("p j t -> p (j t)"),
+            )
+
+        def stage1(q):
+            d_codes = work2.tile([P, 2, 512], U32, tag="d_codes", align_bytes=64)
+            d_scales = work2.tile([P, 2, 512], U8, tag="d_scales", align_bytes=64)
+            for g in range(2):
+                y = work3.tile([P, 4, 512], F32, tag="y")
+                for t in range(4):
+                    ct = 4 * g + t
+                    acc = ps_1.tile([P, 512], F32, tag="acc1")
+                    nc.tensor.matmul_mx(
+                        out=acc[:],
+                        lhsT=c_codes[:, 128 * ct : 128 * ct + 128].bitcast(FP8X4),
+                        lhsT_scale=c_scales[:, 128 * ct : 128 * ct + 128],
+                        rhs=x_codes[:, 512 * q : 512 * q + 512].bitcast(FP8X4),
+                        rhs_scale=x_scales[:, 512 * q : 512 * q + 512],
+                        start=True,
+                        stop=True,
+                    )
+                    nc.vector.scalar_tensor_tensor(
+                        out=y[:, t, :],
+                        in0=acc[:],
+                        scalar=c2h[:, ct : ct + 1],
+                        in1=x2hb[:, q, :],
+                        op0=ALU.subtract,
+                        op1=ALU.subtract,
+                    )
+                r = work2.tile([P, 512, 4], F32, tag="r")
+                nc.vector.tensor_scalar_min(
+                    out=r[:], in0=y[:].rearrange("p t n -> p n t"), scalar1=0.0
+                )
+                dg = work2.tile([P, 2048], BF16, tag="dg", align_bytes=64)
+                nc.scalar.activation(
+                    out=dg[:],
+                    in_=r[:].rearrange("p n t -> p (n t)"),
+                    func=ACT.Exp,
+                    scale=g2[:, 0:1],
+                )
+                nc.vector.quantize_mx(
+                    out=d_codes[:, g, :].bitcast(FP8X4), scales=d_scales[:, g, :], in_=dg[:]
+                )
+            return d_codes, d_scales
+
+        def stage2(q, d_codes, d_scales):
+            for a in range(4):
+                o_sb = outp.tile([P, C], F32, tag="o_sb")
+                for jh in range(2):
+                    acc = ps_2.tile([P, 512], F32, tag="acc2")
+                    for g in range(2):
+                        nc.tensor.matmul_mx(
+                            out=acc[:],
+                            lhsT=d_codes[:, g, 128 * a : 128 * a + 128].bitcast(FP8X4),
+                            lhsT_scale=d_scales[:, g, 128 * a : 128 * a + 128],
+                            rhs=n_codes[:, g, 512 * jh : 512 * jh + 512].bitcast(FP8X4),
+                            rhs_scale=n_scales[:, g, 512 * jh : 512 * jh + 512],
+                            start=(g == 0),
+                            stop=(g == 1),
+                        )
+                    nc.scalar.copy(out=o_sb[:, 512 * jh : 512 * jh + 512], in_=acc[:])
+                nc.sync.dma_start(out=o_view[:, 4 * q + a, :], in_=o_sb[:])
+
+        prep_inputs(0)
+        prep_centers(0)
+        prep_centers(1)
+        dens = stage1(0)
+        prep_norm(0)
+        prep_norm(1)
+        for q in range(1, CHUNKS):
+            prep_inputs(q)
+            nxt = stage1(q)
+            stage2(q - 1, dens[0], dens[1])
+            dens = nxt
+        stage2(CHUNKS - 1, dens[0], dens[1])

@@ -15,8 +15,14 @@ N, D, C = 2048, 512, 1024
 P = 128
 FLOPS = 2 * N * D * C + 2 * N * C * C
 
-CHUNKS = 4
-TILES = 4
+CHUNK_TILES = [2, 4, 4, 4, 2]
+FIRST = [sum(CHUNK_TILES[:q]) for q in range(len(CHUNK_TILES))]
+CHUNKS = len(CHUNK_TILES)
+ROOT_HALF = 0.5 ** 0.5
+VE = {2: ["", ""], 3: ["", ""], 4: ["V", ""], 5: ["V", "V"], 6: ["V", ""], 7: ["V", "V"], 8: ["V", "V"], 9: ["V", "V"]}
+SE = {2: ["", "", ""], 3: ["", "", "SS"], 4: ["S", "", ""], 5: ["S", "S", ""], 6: ["S", "S", "S"], 7: ["S", "S", ""], 8: ["S", "S", ""], 9: ["S", "S", ""]}
+SQUARES = {2: [6, 7, 8, 9], 3: [10, 11], 4: [12, 13], 5: [14, 15], 6: [], 7: [], 8: [], 9: []}
+NORM = "VS"
 
 
 def tile_nystroem_kernel(tc, inputs, centers, gamma, normalization, out):
@@ -25,22 +31,23 @@ def tile_nystroem_kernel(tc, inputs, centers, gamma, normalization, out):
         keep = ctx.enter_context(tc.tile_pool(name="keep", bufs=1))
         work2 = ctx.enter_context(tc.tile_pool(name="work2", bufs=2))
         work3 = ctx.enter_context(tc.tile_pool(name="work3", bufs=3))
-        outp = ctx.enter_context(tc.tile_pool(name="outp", bufs=4))
+        junks = ctx.enter_context(tc.tile_pool(name="junks", bufs=4))
+        outp = ctx.enter_context(tc.tile_pool(name="outp", bufs=6))
         ps_t = ctx.enter_context(tc.psum_pool(name="ps_t", bufs=2))
         ps_1 = ctx.enter_context(tc.psum_pool(name="ps_1", bufs=3))
         ps_2 = ctx.enter_context(tc.psum_pool(name="ps_2", bufs=3))
 
-        x_view = inputs.rearrange("(p i) d -> p i d", i=CHUNKS * TILES)
+        x_view = inputs.rearrange("(p i) d -> p i d", i=16)
         c_view = centers.rearrange("(g p t) d -> g p t d", g=2, t=4)
         n_view = normalization.rearrange("(g p t) j -> g p t j", g=2, t=4)
-        o_view = out.rearrange("(p i) j -> p i j", i=CHUNKS * TILES)
+        o_view = out.rearrange("(p i) j -> p i j", i=16)
 
         ident = keep.tile([P, P], F32)
         g_bf = keep.tile([P, 1], BF16)
         g2 = keep.tile([P, 1], F32)
         warm = keep.tile([P, 1], F32)
         c_sb = keep.tile([P, 2, 4, D], BF16)
-        x_sb = keep.tile([P, CHUNKS * TILES, D], BF16)
+        x_sb = keep.tile([P, 16, D], BF16)
         n_raw = keep.tile([P, 2, 4, C], BF16)
         c_codes = keep.tile([P, C], U32, align_bytes=64)
         c_scales = keep.tile([P, C], U8, align_bytes=64)
@@ -48,165 +55,356 @@ def tile_nystroem_kernel(tc, inputs, centers, gamma, normalization, out):
         x_scales = keep.tile([P, N], U8, align_bytes=64)
         n_codes = keep.tile([P, 2, C], U32, align_bytes=64)
         n_scales = keep.tile([P, 2, C], U8, align_bytes=64)
-        x2col = keep.tile([P, CHUNKS * TILES], F32)
-        c2col = keep.tile([P, 8], F32)
+        x2h = keep.tile([P, 16], F32)
         c2h = keep.tile([P, 8], F32)
-        x2hb = keep.tile([P, CHUNKS, 512], F32)
+        x2hb = keep.tile([P, N], F32)
 
         nc.scalar.dma_start(out=g_bf[:], in_=gamma.partition_broadcast(P))
-        nc.sync.dma_start(out=c_sb[:, 0], in_=c_view[0])
-        nc.sync.dma_start(out=x_sb[:, 0:4, :], in_=x_view[:, 0:4, :])
+        nc.sync.dma_start(out=x_sb[:, 0:2, :], in_=x_view[:, 0:2, :])
+        nc.sync.dma_start(out=c_sb[:, 0, 0:2], in_=c_view[0][:, 0:2, :])
+        nc.sync.dma_start(out=c_sb[:, 0, 2:4], in_=c_view[0][:, 2:4, :])
         nc.sync.dma_start(out=c_sb[:, 1], in_=c_view[1])
-        nc.sync.dma_start(out=x_sb[:, 4:8, :], in_=x_view[:, 4:8, :])
+        nc.sync.dma_start(out=x_sb[:, 2:6, :], in_=x_view[:, 2:6, :])
         nc.sync.dma_start(out=n_raw[:, 0], in_=n_view[0])
         nc.sync.dma_start(out=n_raw[:, 1], in_=n_view[1])
-        nc.sync.dma_start(out=x_sb[:, 8:12, :], in_=x_view[:, 8:12, :])
-        nc.sync.dma_start(out=x_sb[:, 12:16, :], in_=x_view[:, 12:16, :])
+        nc.sync.dma_start(out=x_sb[:, 6:10, :], in_=x_view[:, 6:10, :])
+        nc.sync.dma_start(out=x_sb[:, 10:16, :], in_=x_view[:, 10:16, :])
 
         make_identity(nc, ident[:])
         nc.vector.memset(warm[:], 0.0)
         nc.scalar.activation(out=warm[:], in_=warm[:], func=ACT.Exp)
         nc.vector.tensor_scalar_mul(out=g2[:], in0=g_bf[:], scalar1=2.0)
 
-        def transpose_rows(row_tiles, grouped):
+        def transpose_pair(rows):
+            tp = ps_t.tile([P, 2, 256], F32, tag="tp", name="tp")
+            for a in range(2):
+                src = rows[a].bitcast(F32)
+                for u in range(2):
+                    nc.tensor.transpose(
+                        tp[:, u, 128 * a : 128 * a + 128],
+                        src[:, 128 * u : 128 * u + 128],
+                        ident[:],
+                    )
+            return tp
+
+        def transpose_leave(tp, grouped, b):
             words = grouped[:].bitcast(F32).rearrange("p (c u) -> p c u", u=2)
-            for b in range(2):
-                tp = ps_t.tile([P, 2, 256], F32, tag="tp")
-                for a in range(2):
-                    src = row_tiles[2 * b + a].bitcast(F32)
-                    for u in range(2):
-                        nc.tensor.transpose(
-                            tp[:, u, 128 * a : 128 * a + 128],
-                            src[:, 128 * u : 128 * u + 128],
-                            ident[:],
-                        )
-                nc.vector.tensor_copy(
-                    out=words[:, 256 * b : 256 * b + 256, :],
-                    in_=tp[:].rearrange("p u c -> p c u"),
-                )
-
-        def squares(row_tiles, col_tile, first):
-            for a in range(4):
-                junk = work2.tile([P, D], BF16, tag="junk")
-                nc.scalar.activation(
-                    out=junk[:],
-                    in_=row_tiles[a],
-                    func=ACT.Square,
-                    accum_out=col_tile[:, first + a : first + a + 1],
-                )
-
-        def prep_centers(g):
-            rows = [c_sb[:, g, t, :] for t in range(4)]
-            squares(rows, c2col, 4 * g)
-            nc.vector.tensor_scalar_mul(
-                out=c2h[:, 4 * g : 4 * g + 4], in0=c2col[:, 4 * g : 4 * g + 4], scalar1=0.5
+            nc.vector.tensor_copy(
+                out=words[:, 256 * b : 256 * b + 256, :],
+                in_=tp[:].rearrange("p u c -> p c u"),
             )
-            gc = work2.tile([P, 2048], BF16, tag="gc", align_bytes=64)
-            transpose_rows(rows, gc)
+
+        def half_square(row, col):
+            junk = junks.tile([P, D], BF16, tag="junk")
+            nc.scalar.activation(
+                out=junk[:], in_=row, func=ACT.Square, scale=ROOT_HALF, accum_out=col
+            )
+
+        def c_square(g, t):
+            half_square(c_sb[:, g, t, :], c2h[:, 4 * g + t : 4 * g + t + 1])
+
+        def c_transposes(g, b):
+            return transpose_pair([c_sb[:, g, 2 * b, :], c_sb[:, g, 2 * b + 1, :]])
+
+        def c_quantize(g, gc):
             nc.vector.quantize_mx(
                 out=c_codes[:, 512 * g : 512 * g + 512].bitcast(FP8X4),
                 scales=c_scales[:, 512 * g : 512 * g + 512],
                 in_=gc[:],
             )
 
-        def prep_inputs(q):
-            rows = [x_sb[:, 4 * q + a, :] for a in range(4)]
-            squares(rows, x2col, 4 * q)
-            gx = work2.tile([P, 2048], BF16, tag="gx", align_bytes=64)
-            transpose_rows(rows, gx)
-            nc.vector.quantize_mx(
-                out=x_codes[:, 512 * q : 512 * q + 512].bitcast(FP8X4),
-                scales=x_scales[:, 512 * q : 512 * q + 512],
-                in_=gx[:],
-            )
-            rep = work2.tile([P, 4, P], F32, tag="rep")
-            nc.vector.tensor_scalar_mul(
-                out=rep[:],
-                in0=x2col[:, 4 * q : 4 * q + 4].unsqueeze(2).to_broadcast([P, 4, P]),
-                scalar1=0.5,
-            )
-            tpx = ps_t.tile([P, 4, P], F32, tag="tp")
-            for a in range(4):
-                nc.tensor.transpose(tpx[:, a, :], rep[:, a, :], ident[:])
-            nc.scalar.copy(out=x2hb[:, q, :], in_=tpx[:].rearrange("p a c -> p (a c)"))
+        def x_square(i):
+            half_square(x_sb[:, i, :], x2h[:, i : i + 1])
 
-        def prep_norm(g):
-            ng = work2.tile([P, C, 4], BF16, tag="ng", align_bytes=64)
-            nc.vector.tensor_copy(out=ng[:], in_=n_raw[:, g].rearrange("p t j -> p j t"))
+        def x_grouped(q):
+            return work2.tile([P, 512 * CHUNK_TILES[q]], BF16, tag="gx", align_bytes=64, name="gx")
+
+        def x_transposes(q, b):
+            i = FIRST[q] + 2 * b
+            return transpose_pair([x_sb[:, i, :], x_sb[:, i + 1, :]])
+
+        def x_quantize(q, gx):
+            n0, n1 = P * FIRST[q], P * (FIRST[q] + CHUNK_TILES[q])
             nc.vector.quantize_mx(
-                out=n_codes[:, g, :].bitcast(FP8X4),
-                scales=n_scales[:, g, :],
-                in_=ng[:].rearrange("p j t -> p (j t)"),
+                out=x_codes[:, n0:n1].bitcast(FP8X4), scales=x_scales[:, n0:n1], in_=gx[:]
             )
 
-        def stage1(q):
-            d_codes = work2.tile([P, 2, 512], U32, tag="d_codes", align_bytes=64)
-            d_scales = work2.tile([P, 2, 512], U8, tag="d_scales", align_bytes=64)
+        def x_spread(q):
+            nt = CHUNK_TILES[q]
+            tpx = ps_t.tile([P, nt, P], F32, tag="tp", name="tpx")
+            for a in range(nt):
+                i = FIRST[q] + a
+                nc.tensor.transpose(tpx[:, a, :], x2h[:, i : i + 1].to_broadcast([P, P]), ident[:])
+            return tpx
+
+        def x_spread_leave(q, tpx):
+            nt = CHUNK_TILES[q]
+            n0 = P * FIRST[q]
+            nc.scalar.copy(out=x2hb[:, n0 : n0 + P * nt], in_=tpx[:].rearrange("p a c -> p (a c)"))
+
+        def norm_group(g, half, engine):
+            j0 = 512 * half
+            ng = work2.tile([P, 512 * 4], BF16, tag="ng" + engine, align_bytes=64, name="ng")
+            dst = ng[:].rearrange("p (c i t) -> p c t i", i=4, t=4)
+            src = n_raw[:, g, :, j0 : j0 + 512].rearrange("p t (c i) -> p c t i", i=4)
+            if engine == "V":
+                nc.vector.tensor_copy(out=dst, in_=src)
+            else:
+                nc.scalar.copy(out=dst, in_=src)
+            return ng
+
+        def norm_quantize(g, half, ng):
+            j0 = 512 * half
+            nc.vector.quantize_mx(
+                out=n_codes[:, g, j0 : j0 + 512].bitcast(FP8X4),
+                scales=n_scales[:, g, j0 : j0 + 512],
+                in_=ng[:],
+            )
+
+        def m1_issue(q, g, t):
+            ct = 4 * g + t
+            n0, n1 = P * FIRST[q], P * (FIRST[q] + CHUNK_TILES[q])
+            acc = ps_1.tile([P, n1 - n0], F32, tag="acc1", name="acc1")
+            nc.tensor.matmul_mx(
+                out=acc[:],
+                lhsT=c_codes[:, 128 * ct : 128 * ct + 128].bitcast(FP8X4),
+                lhsT_scale=c_scales[:, 128 * ct : 128 * ct + 128],
+                rhs=x_codes[:, n0:n1].bitcast(FP8X4),
+                rhs_scale=x_scales[:, n0:n1],
+                start=True,
+                stop=True,
+            )
+            return acc
+
+        def m1_leave(q, g, t, acc, y):
+            ct = 4 * g + t
+            n0, n1 = P * FIRST[q], P * (FIRST[q] + CHUNK_TILES[q])
+            nc.vector.scalar_tensor_tensor(
+                out=y[:, t, :],
+                in0=acc[:],
+                scalar=c2h[:, ct : ct + 1],
+                in1=x2hb[:, n0:n1],
+                op0=ALU.subtract,
+                op1=ALU.subtract,
+            )
+
+        def y_tile(q):
+            return work3.tile([P, 4, P * CHUNK_TILES[q]], F32, tag="y", name="y")
+
+        def dens_exp(q, y):
+            dg = work3.tile([P, 512 * CHUNK_TILES[q]], BF16, tag="dg", align_bytes=64)
+            nc.scalar.activation(
+                out=dg[:].rearrange("p (c i t) -> p c t i", i=4, t=4),
+                in_=y[:].rearrange("p t (c i) -> p c t i", i=4),
+                func=ACT.Exp,
+                scale=g2[:, 0:1],
+            )
+            return dg
+
+        def dens_clip(dg):
+            nc.vector.tensor_scalar_min(out=dg[:], in0=dg[:], scalar1=1.0)
+
+        def dens_tiles(q):
+            w = P * CHUNK_TILES[q]
+            codes = work3.tile([P, 2, w], U32, tag="d_codes", align_bytes=64, name="d_codes")
+            scales = work3.tile([P, 2, w], U8, tag="d_scales", align_bytes=64, name="d_scales")
+            return codes, scales
+
+        def dens_quantize(g, dg, codes, scales):
+            nc.vector.quantize_mx(
+                out=codes[:, g, :].bitcast(FP8X4), scales=scales[:, g, :], in_=dg[:]
+            )
+
+        o_tiles = {}
+
+        def m2_issue(q, k):
+            codes, scales = dens[q]
+            a, jh = divmod(k, 2)
+            acc = ps_2.tile([P, 512], F32, tag="acc2", name="acc2")
             for g in range(2):
-                y = work3.tile([P, 4, 512], F32, tag="y")
+                nc.tensor.matmul_mx(
+                    out=acc[:],
+                    lhsT=codes[:, g, 128 * a : 128 * a + 128].bitcast(FP8X4),
+                    lhsT_scale=scales[:, g, 128 * a : 128 * a + 128],
+                    rhs=n_codes[:, g, 512 * jh : 512 * jh + 512].bitcast(FP8X4),
+                    rhs_scale=n_scales[:, g, 512 * jh : 512 * jh + 512],
+                    start=(g == 0),
+                    stop=(g == 1),
+                )
+            return acc
+
+        def m2_leave(q, k, acc, engine):
+            a, jh = divmod(k, 2)
+            i = FIRST[q] + a
+            if jh == 0:
+                o_tiles[i] = outp.tile([P, C], F32, tag="o_sb", name="o_sb")
+            dst = o_tiles[i][:, 512 * jh : 512 * jh + 512]
+            if engine == "V":
+                nc.vector.tensor_copy(out=dst, in_=acc[:])
+            else:
+                nc.scalar.copy(out=dst, in_=acc[:])
+            if jh == 1:
+                nc.sync.dma_start(out=o_view[:, i, :], in_=o_tiles[i][:])
+
+        dens = {}
+        y = {}
+        dg = {}
+        steps = [(q, g) for q in range(CHUNKS) for g in range(2)]
+        slots = [(s, t) for s in range(2 * CHUNKS) for t in range(4)]
+        banks = [(q, k) for q in range(CHUNKS) for k in range(2 * CHUNK_TILES[q])]
+        acc1 = []
+        acc2 = []
+        left1 = []
+        left2 = []
+
+        def issue1(upto):
+            while len(acc1) < min(upto, len(slots)):
+                s, t = slots[len(acc1)]
+                acc1.append(m1_issue(steps[s][0], steps[s][1], t))
+
+        def leave1():
+            s, t = slots[len(left1)]
+            if t == 0:
+                y[s] = y_tile(steps[s][0])
+            m1_leave(steps[s][0], steps[s][1], t, acc1[len(left1)], y[s])
+            left1.append(s)
+
+        def issue2(upto):
+            while len(acc2) < min(upto, len(banks)):
+                q, k = banks[len(acc2)]
+                acc2.append(m2_issue(q, k))
+
+        def leave2(engines, ready):
+            for engine in engines:
+                if len(left2) < len(banks):
+                    issue2(len(left2) + 1)
+                    q, k = banks[len(left2)]
+                    m2_leave(q, k, acc2[len(left2)], engine)
+                    left2.append(k)
+                    issue2(min(len(left2) + 2, ready))
+
+        def quantize_step(s):
+            q, g = steps[s]
+            if g == 0:
+                dens[q] = dens_tiles(q)
+            dens_quantize(g, dg[s], dens[q][0], dens[q][1])
+
+        def ready_banks(s):
+            q = steps[s][0] + steps[s][1]
+            return 2 * sum(CHUNK_TILES[:q])
+
+        gx = {}
+        tps = {}
+        ng = {}
+
+        def run():
+            gc0 = work2.tile([P, 2048], BF16, tag="gc", align_bytes=64, name="gc")
+            gc1 = work2.tile([P, 2048], BF16, tag="gc", align_bytes=64, name="gc")
+            gx[0] = x_grouped(0)
+            gx[1] = x_grouped(1)
+            tx = x_transposes(0, 0)
+            ta = c_transposes(0, 0)
+            x_square(0)
+            transpose_leave(tx, gx[0], 0)
+            x_square(1)
+            transpose_leave(ta, gc0, 0)
+            tb = c_transposes(0, 1)
+            sp = x_spread(0)
+            x_quantize(0, gx[0])
+            transpose_leave(tb, gc0, 1)
+            c_square(0, 0)
+            x_spread_leave(0, sp)
+            for t in range(1, 4):
+                c_square(0, t)
+            ta = c_transposes(1, 0)
+            c_quantize(0, gc0)
+            issue1(3)
+            transpose_leave(ta, gc1, 0)
+            tb = c_transposes(1, 1)
+            leave1()
+            issue1(4)
+            leave1()
+            leave1()
+            transpose_leave(tb, gc1, 1)
+            leave1()
+            for t in range(4):
+                c_square(1, t)
+            ta = x_transposes(1, 0)
+            tb = x_transposes(1, 1)
+            c_quantize(1, gc1)
+            issue1(7)
+            dg[0] = dens_exp(0, y[0])
+            for i in range(2, 6):
+                x_square(i)
+            transpose_leave(ta, gx[1], 0)
+            transpose_leave(tb, gx[1], 1)
+            leave1()
+            issue1(8)
+            x_quantize(1, gx[1])
+            leave1()
+            dens_clip(dg[0])
+            leave1()
+            leave1()
+            sp = x_spread(1)
+            x_spread_leave(1, sp)
+            quantize_step(0)
+            issue1(10)
+
+            for s in range(2, len(steps)):
+                q, g = steps[s]
+                nt = CHUNK_TILES[q + 1] if q + 1 < CHUNKS else 0
+                if nt and g == 0:
+                    gx[q + 1] = x_grouped(q + 1)
+                old = ready_banks(s - 2)
                 for t in range(4):
-                    ct = 4 * g + t
-                    acc = ps_1.tile([P, 512], F32, tag="acc1")
-                    nc.tensor.matmul_mx(
-                        out=acc[:],
-                        lhsT=c_codes[:, 128 * ct : 128 * ct + 128].bitcast(FP8X4),
-                        lhsT_scale=c_scales[:, 128 * ct : 128 * ct + 128],
-                        rhs=x_codes[:, 512 * q : 512 * q + 512].bitcast(FP8X4),
-                        rhs_scale=x_scales[:, 512 * q : 512 * q + 512],
-                        start=True,
-                        stop=True,
-                    )
-                    nc.vector.scalar_tensor_tensor(
-                        out=y[:, t, :],
-                        in0=acc[:],
-                        scalar=c2h[:, ct : ct + 1],
-                        in1=x2hb[:, q, :],
-                        op0=ALU.subtract,
-                        op1=ALU.subtract,
-                    )
-                r = work2.tile([P, 512, 4], F32, tag="r")
-                nc.vector.tensor_scalar_min(
-                    out=r[:], in0=y[:].rearrange("p t n -> p n t"), scalar1=0.0
-                )
-                dg = work2.tile([P, 2048], BF16, tag="dg", align_bytes=64)
-                nc.scalar.activation(
-                    out=dg[:],
-                    in_=r[:].rearrange("p n t -> p (n t)"),
-                    func=ACT.Exp,
-                    scale=g2[:, 0:1],
-                )
-                nc.vector.quantize_mx(
-                    out=d_codes[:, g, :].bitcast(FP8X4), scales=d_scales[:, g, :], in_=dg[:]
-                )
-            return d_codes, d_scales
+                    leave1()
+                    issue1(len(left1) + 2)
+                    if t == 0:
+                        dg[s - 1] = dens_exp(steps[s - 1][0], y[s - 1])
+                        leave2(VE[s][0], old)
+                        if nt and g == 0:
+                            tps[0] = x_transposes(q + 1, 0)
+                        if nt and g == 1:
+                            sp = x_spread(q + 1)
+                        if s in (2, 3):
+                            ng[0] = norm_group(0, s - 2, NORM[0])
+                    if t == 1:
+                        if nt and g == 0:
+                            transpose_leave(tps[0], gx[q + 1], 0)
+                        if nt and g == 1:
+                            x_quantize(q + 1, gx[q + 1])
+                            x_spread_leave(q + 1, sp)
+                        if s in (2, 3):
+                            ng[1] = norm_group(1, s - 2, NORM[1])
+                            norm_quantize(0, s - 2, ng[0])
+                        if nt == 4 and g == 0:
+                            tps[1] = x_transposes(q + 1, 1)
+                        leave2(SE[s][0], old)
+                    if t == 2:
+                        dens_clip(dg[s - 1])
+                        for i in SQUARES[s][:2]:
+                            x_square(i)
+                        leave2(SE[s][1], old)
+                    if t == 3:
+                        if nt == 4 and g == 0:
+                            transpose_leave(tps[1], gx[q + 1], 1)
+                        leave2(VE[s][1], old)
+                        quantize_step(s - 1)
+                        if s in (2, 3):
+                            norm_quantize(1, s - 2, ng[1])
+                        for i in SQUARES[s][2:]:
+                            x_square(i)
+                        leave2(SE[s][2], old)
 
-        def stage2(q, d_codes, d_scales):
-            for a in range(4):
-                o_sb = outp.tile([P, C], F32, tag="o_sb")
-                for jh in range(2):
-                    acc = ps_2.tile([P, 512], F32, tag="acc2")
-                    for g in range(2):
-                        nc.tensor.matmul_mx(
-                            out=acc[:],
-                            lhsT=d_codes[:, g, 128 * a : 128 * a + 128].bitcast(FP8X4),
-                            lhsT_scale=d_scales[:, g, 128 * a : 128 * a + 128],
-                            rhs=n_codes[:, g, 512 * jh : 512 * jh + 512].bitcast(FP8X4),
-                            rhs_scale=n_scales[:, g, 512 * jh : 512 * jh + 512],
-                            start=(g == 0),
-                            stop=(g == 1),
-                        )
-                    nc.scalar.copy(out=o_sb[:, 512 * jh : 512 * jh + 512], in_=acc[:])
-                nc.sync.dma_start(out=o_view[:, 4 * q + a, :], in_=o_sb[:])
+            s = len(steps)
+            dg[s - 1] = dens_exp(CHUNKS - 1, y[s - 1])
+            leave2("VVS", ready_banks(s - 2))
+            dens_clip(dg[s - 1])
+            leave2("V", ready_banks(s - 2))
+            quantize_step(s - 1)
+            leave2("SVSVSVSVSV", len(banks))
 
-        prep_inputs(0)
-        prep_centers(0)
-        prep_centers(1)
-        dens = stage1(0)
-        prep_norm(0)
-        prep_norm(1)
-        for q in range(1, CHUNKS):
-            prep_inputs(q)
-            nxt = stage1(q)
-            stage2(q - 1, dens[0], dens[1])
-            dens = nxt
-        stage2(CHUNKS - 1, dens[0], dens[1])
+        with tc.manual_schedule(
+            engines={mybir.EngineType.DVE, mybir.EngineType.Activation, mybir.EngineType.PE}
+        ):
+            run()

@@ -15,14 +15,24 @@ N, D, C = 2048, 512, 1024
 P = 128
 FLOPS = 2 * N * D * C + 2 * N * C * C
 
-CHUNK_TILES = [2, 4, 4, 4, 2]
+CHUNK_TILES = [2,4,4,4,2]
 FIRST = [sum(CHUNK_TILES[:q]) for q in range(len(CHUNK_TILES))]
 CHUNKS = len(CHUNK_TILES)
 ROOT_HALF = 0.5 ** 0.5
-VE = {2: ["", ""], 3: ["", ""], 4: ["V", ""], 5: ["V", "V"], 6: ["V", ""], 7: ["V", "V"], 8: ["V", "V"], 9: ["V", "V"]}
-SE = {2: ["", "", ""], 3: ["", "", "SS"], 4: ["S", "", ""], 5: ["S", "S", ""], 6: ["S", "S", "S"], 7: ["S", "S", ""], 8: ["S", "S", ""], 9: ["S", "S", ""]}
-SQUARES = {2: [6, 7, 8, 9], 3: [10, 11], 4: [12, 13], 5: [14, 15], 6: [], 7: [], 8: [], 9: []}
-NORM = "VS"
+SLOT = {2: ["", "", "", ""], 3: ["", "", "", "S"], 4: ["", "", "S", "S"], 5: ["V", "", "SS", "S"], 6: ["V", "", "SS", "S"], 7: ["V", "", "SS", "S"], 8: ["V", "", "SS", "S"], 9: ["V", "", "SS", "S"]}
+NSLOT = {2: [1, 0, 0, 1], 3: [0, 1, 0, 1], 4: [0, 0, 0, 0], 5: [0, 0, 0, 0], 6: [0, 0, 0, 0], 7: [0, 0, 0, 0], 8: [0, 0, 0, 0], 9: [0, 0, 0, 0]}
+NORM = "VSVS"
+NORM_ORDER = [(0, 0), (1, 0), (0, 1), (1, 1)]
+TAIL = ["VSVS", "VS", "VSVS"]
+LAG = 2
+LEAD = 2
+SC = 4
+SX = 4
+LAST = 4
+TC1 = "VV"
+TX1 = "VV"
+TX = "VV"
+GRAM = [0,0,0,0,0]
 
 
 def tile_nystroem_kernel(tc, inputs, centers, gamma, normalization, out):
@@ -31,6 +41,7 @@ def tile_nystroem_kernel(tc, inputs, centers, gamma, normalization, out):
         keep = ctx.enter_context(tc.tile_pool(name="keep", bufs=1))
         work2 = ctx.enter_context(tc.tile_pool(name="work2", bufs=2))
         work3 = ctx.enter_context(tc.tile_pool(name="work3", bufs=3))
+        work4 = ctx.enter_context(tc.tile_pool(name="work4", bufs=4))
         junks = ctx.enter_context(tc.tile_pool(name="junks", bufs=4))
         outp = ctx.enter_context(tc.tile_pool(name="outp", bufs=6))
         ps_t = ctx.enter_context(tc.psum_pool(name="ps_t", bufs=2))
@@ -87,24 +98,61 @@ def tile_nystroem_kernel(tc, inputs, centers, gamma, normalization, out):
                     )
             return tp
 
-        def transpose_leave(tp, grouped, b):
+        def transpose_leave(tp, grouped, b, engine="V"):
             words = grouped[:].bitcast(F32).rearrange("p (c u) -> p c u", u=2)
-            nc.vector.tensor_copy(
-                out=words[:, 256 * b : 256 * b + 256, :],
-                in_=tp[:].rearrange("p u c -> p c u"),
-            )
+            dst = words[:, 256 * b : 256 * b + 256, :]
+            src = tp[:].rearrange("p u c -> p c u")
+            if engine == "V":
+                nc.vector.tensor_copy(out=dst, in_=src)
+            else:
+                nc.scalar.copy(out=dst, in_=src)
 
-        def half_square(row, col):
-            junk = junks.tile([P, D], BF16, tag="junk")
-            nc.scalar.activation(
-                out=junk[:], in_=row, func=ACT.Square, scale=ROOT_HALF, accum_out=col
-            )
+        def half_square(row, col, engine="S"):
+            junk = junks.tile([P, D], BF16, tag="junk" + engine, name="junk")
+            if engine == "S":
+                nc.scalar.activation(
+                    out=junk[:], in_=row, func=ACT.Square, scale=ROOT_HALF, accum_out=col
+                )
+            else:
+                nc.vector.scalar_tensor_tensor(
+                    out=junk[:],
+                    in0=row,
+                    scalar=0.5,
+                    in1=row,
+                    op0=ALU.mult,
+                    op1=ALU.mult,
+                    accum_out=col,
+                )
 
-        def c_square(g, t):
-            half_square(c_sb[:, g, t, :], c2h[:, 4 * g + t : 4 * g + t + 1])
+        def c_square(g, t, engine="S"):
+            half_square(c_sb[:, g, t, :], c2h[:, 4 * g + t : 4 * g + t + 1], engine)
 
         def c_transposes(g, b):
             return transpose_pair([c_sb[:, g, 2 * b, :], c_sb[:, g, 2 * b + 1, :]])
+
+        def gram(grouped, tiles, cols):
+            rows = grouped[:].rearrange("p (n t) -> p t n", t=4)
+            prod = ps_t.tile([P, len(tiles), P], F32, tag="tp", name="prod")
+            for j, a in enumerate(tiles):
+                for t in range(4):
+                    side = rows[:, t, 128 * a : 128 * a + 128]
+                    nc.tensor.matmul(
+                        prod[:, j, :], lhsT=side, rhs=side, start=(t == 0), stop=(t == 3)
+                    )
+            return prod
+
+        def gram_leave(prod, tiles, col_tile, first):
+            for j, a in enumerate(tiles):
+                junk = junks.tile([P, P], F32, tag="junkG", name="junk")
+                nc.vector.scalar_tensor_tensor(
+                    out=junk[:],
+                    in0=prod[:, j, :],
+                    scalar=0.5,
+                    in1=ident[:],
+                    op0=ALU.mult,
+                    op1=ALU.mult,
+                    accum_out=col_tile[:, first + a : first + a + 1],
+                )
 
         def c_quantize(g, gc):
             nc.vector.quantize_mx(
@@ -144,7 +192,7 @@ def tile_nystroem_kernel(tc, inputs, centers, gamma, normalization, out):
 
         def norm_group(g, half, engine):
             j0 = 512 * half
-            ng = work2.tile([P, 512 * 4], BF16, tag="ng" + engine, align_bytes=64, name="ng")
+            ng = work4.tile([P, 512 * 4], BF16, tag="ng", align_bytes=64, name="ng")
             dst = ng[:].rearrange("p (c i t) -> p c t i", i=4, t=4)
             src = n_raw[:, g, :, j0 : j0 + 512].rearrange("p t (c i) -> p c t i", i=4)
             if engine == "V":
@@ -201,8 +249,13 @@ def tile_nystroem_kernel(tc, inputs, centers, gamma, normalization, out):
             )
             return dg
 
-        def dens_clip(dg):
-            nc.vector.tensor_scalar_min(out=dg[:], in0=dg[:], scalar1=1.0)
+        def dens_clip(dg, engine):
+            if engine == "V":
+                nc.vector.tensor_scalar_min(out=dg[:], in0=dg[:], scalar1=1.0)
+            else:
+                nc.gpsimd.tensor_scalar(
+                    out=dg[:], in0=dg[:], scalar1=1.0, scalar2=0.0, op0=ALU.min, op1=ALU.max
+                )
 
         def dens_tiles(q):
             w = P * CHUNK_TILES[q]
@@ -217,20 +270,23 @@ def tile_nystroem_kernel(tc, inputs, centers, gamma, normalization, out):
 
         o_tiles = {}
 
-        def m2_issue(q, k):
+        def m2_pass(acc, q, k, g):
             codes, scales = dens[q]
             a, jh = divmod(k, 2)
+            nc.tensor.matmul_mx(
+                out=acc[:],
+                lhsT=codes[:, g, 128 * a : 128 * a + 128].bitcast(FP8X4),
+                lhsT_scale=scales[:, g, 128 * a : 128 * a + 128],
+                rhs=n_codes[:, g, 512 * jh : 512 * jh + 512].bitcast(FP8X4),
+                rhs_scale=n_scales[:, g, 512 * jh : 512 * jh + 512],
+                start=(g == 0),
+                stop=(g == 1),
+            )
+
+        def m2_issue(q, k):
             acc = ps_2.tile([P, 512], F32, tag="acc2", name="acc2")
             for g in range(2):
-                nc.tensor.matmul_mx(
-                    out=acc[:],
-                    lhsT=codes[:, g, 128 * a : 128 * a + 128].bitcast(FP8X4),
-                    lhsT_scale=scales[:, g, 128 * a : 128 * a + 128],
-                    rhs=n_codes[:, g, 512 * jh : 512 * jh + 512].bitcast(FP8X4),
-                    rhs_scale=n_scales[:, g, 512 * jh : 512 * jh + 512],
-                    start=(g == 0),
-                    stop=(g == 1),
-                )
+                m2_pass(acc, q, k, g)
             return acc
 
         def m2_leave(q, k, acc, engine):
@@ -243,7 +299,9 @@ def tile_nystroem_kernel(tc, inputs, centers, gamma, normalization, out):
                 nc.vector.tensor_copy(out=dst, in_=acc[:])
             else:
                 nc.scalar.copy(out=dst, in_=acc[:])
-            if jh == 1:
+            if q == CHUNKS - 1:
+                nc.sync.dma_start(out=o_view[:, i, 512 * jh : 512 * jh + 512], in_=dst)
+            elif jh == 1:
                 nc.sync.dma_start(out=o_view[:, i, :], in_=o_tiles[i][:])
 
         dens = {}
@@ -256,6 +314,8 @@ def tile_nystroem_kernel(tc, inputs, centers, gamma, normalization, out):
         acc2 = []
         left1 = []
         left2 = []
+        done = []
+        history = [0]
 
         def issue1(upto):
             while len(acc1) < min(upto, len(slots)):
@@ -270,34 +330,62 @@ def tile_nystroem_kernel(tc, inputs, centers, gamma, normalization, out):
             left1.append(s)
 
         def issue2(upto):
-            while len(acc2) < min(upto, len(banks)):
+            while len(acc2) < min(upto, len(banks) - LAST):
                 q, k = banks[len(acc2)]
                 acc2.append(m2_issue(q, k))
 
-        def leave2(engines, ready):
+        def leave2(engines, lag):
+            ready = history[max(len(history) - 1 - lag, 0)]
             for engine in engines:
-                if len(left2) < len(banks):
+                if len(left2) < min(ready, len(banks) - LAST):
                     issue2(len(left2) + 1)
                     q, k = banks[len(left2)]
                     m2_leave(q, k, acc2[len(left2)], engine)
-                    left2.append(k)
-                    issue2(min(len(left2) + 2, ready))
+                    left2.append(engine)
+                    issue2(min(len(left2) + LEAD, ready))
 
         def quantize_step(s):
             q, g = steps[s]
             if g == 0:
                 dens[q] = dens_tiles(q)
             dens_quantize(g, dg[s], dens[q][0], dens[q][1])
+            done.append(s)
 
-        def ready_banks(s):
-            q = steps[s][0] + steps[s][1]
-            return 2 * sum(CHUNK_TILES[:q])
+        def tick():
+            n = 0
+            if normed:
+                for q, g in [steps[s] for s in done if steps[s][1] == 1]:
+                    n += 2 * CHUNK_TILES[q]
+            history.append(n)
+
+        squares = {s: [] for s in range(2, len(steps))}
+        for q in range(2, CHUNKS):
+            tiles = list(range(FIRST[q], FIRST[q] + CHUNK_TILES[q]))
+            if not GRAM[q]:
+                early = 0 if q == 2 else len(tiles) // 2
+                if early:
+                    squares[2 * q - 3] = squares[2 * q - 3] + tiles[:early]
+                squares[2 * q - 2] = squares[2 * q - 2] + tiles[early:]
 
         gx = {}
         tps = {}
         ng = {}
+        normed = []
 
-        def run():
+        pieces = []
+
+        def norm_piece(k):
+            if k < 4:
+                gg, half = NORM_ORDER[k]
+                pieces.append(norm_group(gg, half, NORM[k]))
+            if 1 <= k <= 4:
+                gg, half = NORM_ORDER[k - 1]
+                norm_quantize(gg, half, pieces[k - 1])
+            if k == 4:
+                pieces.append(0)
+                normed.append(0)
+
+        def head():
             gc0 = work2.tile([P, 2048], BF16, tag="gc", align_bytes=64, name="gc")
             gc1 = work2.tile([P, 2048], BF16, tag="gc", align_bytes=64, name="gc")
             gx[0] = x_grouped(0)
@@ -319,92 +407,119 @@ def tile_nystroem_kernel(tc, inputs, centers, gamma, normalization, out):
             ta = c_transposes(1, 0)
             c_quantize(0, gc0)
             issue1(3)
-            transpose_leave(ta, gc1, 0)
+            transpose_leave(ta, gc1, 0, TC1[0])
             tb = c_transposes(1, 1)
             leave1()
             issue1(4)
             leave1()
             leave1()
-            transpose_leave(tb, gc1, 1)
+            transpose_leave(tb, gc1, 1, TC1[1])
             leave1()
-            for t in range(4):
+            for t in range(SC):
                 c_square(1, t)
             ta = x_transposes(1, 0)
-            tb = x_transposes(1, 1)
             c_quantize(1, gc1)
+            if SC < 4:
+                pc = gram(gc1, range(SC, 4), 4)
             issue1(7)
             dg[0] = dens_exp(0, y[0])
-            for i in range(2, 6):
-                x_square(i)
-            transpose_leave(ta, gx[1], 0)
-            transpose_leave(tb, gx[1], 1)
+            transpose_leave(ta, gx[1], 0, TX1[0])
+            tb = x_transposes(1, 1)
+            if SC < 4:
+                gram_leave(pc, range(SC, 4), c2h, 4)
+            transpose_leave(tb, gx[1], 1, TX1[1])
+            if SX < 4:
+                px = gram(gx[1], range(SX, 4), 0)
+            for i in range(SX):
+                x_square(FIRST[1] + i)
             leave1()
             issue1(8)
             x_quantize(1, gx[1])
             leave1()
-            dens_clip(dg[0])
-            leave1()
+            if SX < 4:
+                gram_leave(px, range(SX, 4), x2h, FIRST[1])
             leave1()
             sp = x_spread(1)
+            leave1()
             x_spread_leave(1, sp)
-            quantize_step(0)
+            dens_clip(dg[0], "V")
             issue1(10)
+            norm_piece(0)
+            quantize_step(0)
 
+
+        def run():
             for s in range(2, len(steps)):
                 q, g = steps[s]
                 nt = CHUNK_TILES[q + 1] if q + 1 < CHUNKS else 0
                 if nt and g == 0:
                     gx[q + 1] = x_grouped(q + 1)
-                old = ready_banks(s - 2)
                 for t in range(4):
                     leave1()
                     issue1(len(left1) + 2)
                     if t == 0:
                         dg[s - 1] = dens_exp(steps[s - 1][0], y[s - 1])
-                        leave2(VE[s][0], old)
                         if nt and g == 0:
                             tps[0] = x_transposes(q + 1, 0)
-                        if nt and g == 1:
-                            sp = x_spread(q + 1)
-                        if s in (2, 3):
-                            ng[0] = norm_group(0, s - 2, NORM[0])
+                        if nt == 4 and g == 1 and GRAM[q + 1]:
+                            tps[1] = gram(gx[q + 1], range(2, 4), 0)
                     if t == 1:
                         if nt and g == 0:
-                            transpose_leave(tps[0], gx[q + 1], 0)
+                            transpose_leave(tps[0], gx[q + 1], 0, TX[0])
                         if nt and g == 1:
                             x_quantize(q + 1, gx[q + 1])
-                            x_spread_leave(q + 1, sp)
-                        if s in (2, 3):
-                            ng[1] = norm_group(1, s - 2, NORM[1])
-                            norm_quantize(0, s - 2, ng[0])
                         if nt == 4 and g == 0:
                             tps[1] = x_transposes(q + 1, 1)
-                        leave2(SE[s][0], old)
+                        if nt and g == 0 and GRAM[q + 1]:
+                            tps[0] = gram(gx[q + 1], range(0, 2), 0)
+                        if nt == 4 and g == 1 and GRAM[q + 1]:
+                            gram_leave(tps[1], range(2, 4), x2h, FIRST[q + 1])
                     if t == 2:
-                        dens_clip(dg[s - 1])
-                        for i in SQUARES[s][:2]:
+                        dens_clip(dg[s - 1], "V")
+                        if nt and g == 0 and GRAM[q + 1]:
+                            gram_leave(tps[0], range(0, 2), x2h, FIRST[q + 1])
+                        if nt and g == 1:
+                            sp = x_spread(q + 1)
+                    if t in (1, 2):
+                        for i in squares[s][t - 1 :: 2]:
                             x_square(i)
-                        leave2(SE[s][1], old)
                     if t == 3:
                         if nt == 4 and g == 0:
-                            transpose_leave(tps[1], gx[q + 1], 1)
-                        leave2(VE[s][1], old)
+                            transpose_leave(tps[1], gx[q + 1], 1, TX[1])
                         quantize_step(s - 1)
-                        if s in (2, 3):
-                            norm_quantize(1, s - 2, ng[1])
-                        for i in SQUARES[s][2:]:
-                            x_square(i)
-                        leave2(SE[s][2], old)
+                        if nt and g == 1:
+                            x_spread_leave(q + 1, sp)
+                    leave2(SLOT[s][t], LAG)
+                    if NSLOT[s][t]:
+                        norm_piece(len(pieces))
+                    tick()
 
             s = len(steps)
-            dg[s - 1] = dens_exp(CHUNKS - 1, y[s - 1])
-            leave2("VVS", ready_banks(s - 2))
-            dens_clip(dg[s - 1])
-            leave2("V", ready_banks(s - 2))
+            q = CHUNKS - 1
+            dg[s - 1] = dens_exp(q, y[s - 1])
+            leave2(TAIL[0], 0)
+            last = [
+                (ps_1 if k < 3 else ps_2).tile([P, 512], F32, tag="acc1" if k < 3 else "acc2", name="last")
+                for k in range(LAST)
+            ]
+            for k in range(LAST):
+                m2_pass(last[k], q, k, 0)
+            dens_clip(dg[s - 1], "V")
+            leave2(TAIL[1], 0)
             quantize_step(s - 1)
-            leave2("SVSVSVSVSV", len(banks))
+            leave2(TAIL[2], 0)
+            for k in range(LAST):
+                m2_pass(last[k], q, k, 1)
+            for k in range(LAST):
+                m2_leave(q, k, last[k], "SV"[k % 2])
+            assert len(left2) + LAST == len(banks), len(left2)
 
         with tc.manual_schedule(
-            engines={mybir.EngineType.DVE, mybir.EngineType.Activation, mybir.EngineType.PE}
+            engines={
+                mybir.EngineType.DVE,
+                mybir.EngineType.Activation,
+                mybir.EngineType.PE,
+            }
         ):
-            run()
+            head()
+        run()

@@ -19,9 +19,9 @@ CHUNK_TILES = [2,4,4,4,2]
 FIRST = [sum(CHUNK_TILES[:q]) for q in range(len(CHUNK_TILES))]
 CHUNKS = len(CHUNK_TILES)
 ROOT_HALF = 0.5 ** 0.5
-SLOT = {2: ["", "", "", ""], 3: ["", "", "", "S"], 4: ["", "", "S", "S"], 5: ["V", "", "SS", "S"], 6: ["V", "", "SS", "S"], 7: ["V", "", "SS", "S"], 8: ["V", "", "SS", "S"], 9: ["V", "", "SS", "S"]}
-NSLOT = {2: [1, 0, 0, 1], 3: [0, 1, 0, 1], 4: [0, 0, 0, 0], 5: [0, 0, 0, 0], 6: [0, 0, 0, 0], 7: [0, 0, 0, 0], 8: [0, 0, 0, 0], 9: [0, 0, 0, 0]}
-NORM = "VSVS"
+SLOT = {2: ["", "", "", ""], 3: ["", "", "", "S"], 4: ["", "", "S", "S"], 5: ["V", "", "SS", "S"], 6: ["V", "", "SS", "S"], 7: ["V", "", "SS", "SV"], 8: ["V", "", "SS", "SV"], 9: ["V", "", "SS", "SV"]}
+NSLOT = {2: [1, 0, 1, 0], 3: [1, 0, 1, 0], 4: [0, 0, 0, 0], 5: [0, 0, 0, 0], 6: [0, 0, 0, 0], 7: [0, 0, 0, 0], 8: [0, 0, 0, 0], 9: [0, 0, 0, 0]}
+NORM = "VVVV"
 NORM_ORDER = [(0, 0), (1, 0), (0, 1), (1, 1)]
 TAIL = ["VSVS", "VS", "VSVS"]
 LAG = 2
@@ -30,8 +30,8 @@ SC = 4
 SX = 4
 LAST = 4
 TC1 = "VV"
-TX1 = "VV"
-TX = "VV"
+TX1 = "VS"
+TX = "SS"
 GRAM = [0,0,0,0,0]
 
 

@@ -84,8 +84,6 @@ def tile_nystroem_kernel(tc, inputs, centers, gamma, normalization, out):
         make_identity(nc, ident[:])
         nc.vector.memset(warm[:], 0.0)
         nc.scalar.activation(out=warm[:], in_=warm[:], func=ACT.Exp)
-        nc.vector.tensor_scalar_mul(out=g2[:], in0=g_bf[:], scalar1=2.0)
-
         def transpose_pair(rows):
             tp = ps_t.tile([P, 2, 256], F32, tag="tp", name="tp")
             for a in range(2):
@@ -399,13 +397,14 @@ def tile_nystroem_kernel(tc, inputs, centers, gamma, normalization, out):
             tb = c_transposes(0, 1)
             sp = x_spread(0)
             x_quantize(0, gx[0])
-            transpose_leave(tb, gc0, 1)
-            c_square(0, 0)
-            x_spread_leave(0, sp)
-            for t in range(1, 4):
+            for t in range(3):
                 c_square(0, t)
+            transpose_leave(tb, gc0, 1)
+            x_spread_leave(0, sp)
+            c_square(0, 3)
             ta = c_transposes(1, 0)
             c_quantize(0, gc0)
+            nc.vector.tensor_scalar_mul(out=g2[:], in0=g_bf[:], scalar1=2.0)
             issue1(3)
             transpose_leave(ta, gc1, 0, TC1[0])
             tb = c_transposes(1, 1)
@@ -415,34 +414,28 @@ def tile_nystroem_kernel(tc, inputs, centers, gamma, normalization, out):
             leave1()
             transpose_leave(tb, gc1, 1, TC1[1])
             leave1()
-            for t in range(SC):
+            for t in range(4):
                 c_square(1, t)
             ta = x_transposes(1, 0)
             c_quantize(1, gc1)
-            if SC < 4:
-                pc = gram(gc1, range(SC, 4), 4)
             issue1(7)
             dg[0] = dens_exp(0, y[0])
             transpose_leave(ta, gx[1], 0, TX1[0])
             tb = x_transposes(1, 1)
-            if SC < 4:
-                gram_leave(pc, range(SC, 4), c2h, 4)
-            transpose_leave(tb, gx[1], 1, TX1[1])
-            if SX < 4:
-                px = gram(gx[1], range(SX, 4), 0)
-            for i in range(SX):
+            for i in range(2):
                 x_square(FIRST[1] + i)
             leave1()
             issue1(8)
+            leave1()
+            leave1()
+            transpose_leave(tb, gx[1], 1, TX1[1])
+            leave1()
+            for i in range(2, 4):
+                x_square(FIRST[1] + i)
             x_quantize(1, gx[1])
-            leave1()
-            if SX < 4:
-                gram_leave(px, range(SX, 4), x2h, FIRST[1])
-            leave1()
             sp = x_spread(1)
-            leave1()
-            x_spread_leave(1, sp)
             dens_clip(dg[0], "V")
+            x_spread_leave(1, sp)
             issue1(10)
             norm_piece(0)
             quantize_step(0)

@@ -19,7 +19,7 @@ CHUNK_TILES = [2,4,4,4,2]
 FIRST = [sum(CHUNK_TILES[:q]) for q in range(len(CHUNK_TILES))]
 CHUNKS = len(CHUNK_TILES)
 ROOT_HALF = 0.5 ** 0.5
-SLOT = {2: ["", "", "", ""], 3: ["", "", "", "S"], 4: ["", "", "S", "S"], 5: ["V", "", "SS", "S"], 6: ["V", "", "SS", "S"], 7: ["V", "", "SS", "SV"], 8: ["V", "", "SS", "SV"], 9: ["V", "", "SS", "SV"]}
+SLOT = {2: ["", "", "", ""], 3: ["", "", "", "S"], 4: ["", "", "S", "S"], 5: ["V", "", "SS", "S"], 6: ["V", "", "SS", "S"], 7: ["V", "", "SS", "SV"], 8: ["V", "", "SS", "SV"], 9: ["V", "", "SV", "SV"]}
 NSLOT = {2: [1, 0, 1, 0], 3: [1, 0, 1, 0], 4: [0, 0, 0, 0], 5: [0, 0, 0, 0], 6: [0, 0, 0, 0], 7: [0, 0, 0, 0], 8: [0, 0, 0, 0], 9: [0, 0, 0, 0]}
 NORM = "VVVV"
 NORM_ORDER = [(0, 0), (1, 0), (0, 1), (1, 1)]
@@ -71,7 +71,8 @@ def tile_nystroem_kernel(tc, inputs, centers, gamma, normalization, out):
         x2hb = keep.tile([P, N], F32)
 
         nc.scalar.dma_start(out=g_bf[:], in_=gamma.partition_broadcast(P))
-        nc.sync.dma_start(out=x_sb[:, 0:2, :], in_=x_view[:, 0:2, :])
+        nc.sync.dma_start(out=x_sb[:, 0:1, :], in_=x_view[:, 0:1, :])
+        nc.sync.dma_start(out=x_sb[:, 1:2, :], in_=x_view[:, 1:2, :])
         nc.sync.dma_start(out=c_sb[:, 0, 0:2], in_=c_view[0][:, 0:2, :])
         nc.sync.dma_start(out=c_sb[:, 0, 2:4], in_=c_view[0][:, 2:4, :])
         nc.sync.dma_start(out=c_sb[:, 1], in_=c_view[1])
@@ -85,8 +86,8 @@ def tile_nystroem_kernel(tc, inputs, centers, gamma, normalization, out):
         nc.vector.memset(warm[:], 0.0)
         nc.scalar.activation(out=warm[:], in_=warm[:], func=ACT.Exp)
         def transpose_pair(rows):
-            tp = ps_t.tile([P, 2, 256], F32, tag="tp", name="tp")
-            for a in range(2):
+            tp = ps_t.tile([P, 2, 128 * len(rows)], F32, tag="tp", name="tp")
+            for a in range(len(rows)):
                 src = rows[a].bitcast(F32)
                 for u in range(2):
                     nc.tensor.transpose(
@@ -96,9 +97,9 @@ def tile_nystroem_kernel(tc, inputs, centers, gamma, normalization, out):
                     )
             return tp
 
-        def transpose_leave(tp, grouped, b, engine="V"):
+        def transpose_leave(tp, grouped, b, engine="V", a=0):
             words = grouped[:].bitcast(F32).rearrange("p (c u) -> p c u", u=2)
-            dst = words[:, 256 * b : 256 * b + 256, :]
+            dst = words[:, 256 * b + 128 * a : 256 * b + 128 * a + tp.shape[2], :]
             src = tp[:].rearrange("p u c -> p c u")
             if engine == "V":
                 nc.vector.tensor_copy(out=dst, in_=src)
@@ -388,10 +389,12 @@ def tile_nystroem_kernel(tc, inputs, centers, gamma, normalization, out):
             gc1 = work2.tile([P, 2048], BF16, tag="gc", align_bytes=64, name="gc")
             gx[0] = x_grouped(0)
             gx[1] = x_grouped(1)
-            tx = x_transposes(0, 0)
-            ta = c_transposes(0, 0)
+            tx = transpose_pair([x_sb[:, 0, :]])
+            ty = transpose_pair([x_sb[:, 1, :]])
             x_square(0)
             transpose_leave(tx, gx[0], 0)
+            ta = c_transposes(0, 0)
+            transpose_leave(ty, gx[0], 0, a=1)
             x_square(1)
             transpose_leave(ta, gc0, 0)
             tb = c_transposes(0, 1)
@@ -495,13 +498,15 @@ def tile_nystroem_kernel(tc, inputs, centers, gamma, normalization, out):
                 (ps_1 if k < 3 else ps_2).tile([P, 512], F32, tag="acc1" if k < 3 else "acc2", name="last")
                 for k in range(LAST)
             ]
-            for k in range(LAST):
+            for k in range(2):
                 m2_pass(last[k], q, k, 0)
             dens_clip(dg[s - 1], "V")
             leave2(TAIL[1], 0)
             quantize_step(s - 1)
             leave2(TAIL[2], 0)
             for k in range(LAST):
+                if k >= 2:
+                    m2_pass(last[k], q, k, 0)
                 m2_pass(last[k], q, k, 1)
             for k in range(LAST):
                 m2_leave(q, k, last[k], "SV"[k % 2])

@@ -19,7 +19,7 @@ CHUNK_TILES = [2,4,4,4,2]
 FIRST = [sum(CHUNK_TILES[:q]) for q in range(len(CHUNK_TILES))]
 CHUNKS = len(CHUNK_TILES)
 ROOT_HALF = 0.5 ** 0.5
-SLOT = {2: ["", "", "", ""], 3: ["", "", "", "S"], 4: ["", "", "S", "S"], 5: ["V", "", "SS", "S"], 6: ["V", "", "SS", "S"], 7: ["V", "", "SS", "SV"], 8: ["V", "", "SS", "SV"], 9: ["V", "", "SV", "SV"]}
+SLOT = {2: ["", "", "", ""], 3: ["", "", "", "S"], 4: ["", "", "S", "S"], 5: ["V", "", "SS", "S"], 6: ["V", "", "SS", "S"], 7: ["V", "", "SS", "SV"], 8: ["V", "", "SS", "SV"], 9: ["V", "", "SS", "SV"]}
 NSLOT = {2: [1, 0, 1, 0], 3: [1, 0, 1, 0], 4: [0, 0, 0, 0], 5: [0, 0, 0, 0], 6: [0, 0, 0, 0], 7: [0, 0, 0, 0], 8: [0, 0, 0, 0], 9: [0, 0, 0, 0]}
 NORM = "VVVV"
 NORM_ORDER = [(0, 0), (1, 0), (0, 1), (1, 1)]
@@ -86,8 +86,8 @@ def tile_nystroem_kernel(tc, inputs, centers, gamma, normalization, out):
         nc.vector.memset(warm[:], 0.0)
         nc.scalar.activation(out=warm[:], in_=warm[:], func=ACT.Exp)
         def transpose_pair(rows):
-            tp = ps_t.tile([P, 2, 128 * len(rows)], F32, tag="tp", name="tp")
-            for a in range(len(rows)):
+            tp = ps_t.tile([P, 2, 256], F32, tag="tp", name="tp")
+            for a in range(2):
                 src = rows[a].bitcast(F32)
                 for u in range(2):
                     nc.tensor.transpose(
@@ -97,9 +97,9 @@ def tile_nystroem_kernel(tc, inputs, centers, gamma, normalization, out):
                     )
             return tp
 
-        def transpose_leave(tp, grouped, b, engine="V", a=0):
+        def transpose_leave(tp, grouped, b, engine="V"):
             words = grouped[:].bitcast(F32).rearrange("p (c u) -> p c u", u=2)
-            dst = words[:, 256 * b + 128 * a : 256 * b + 128 * a + tp.shape[2], :]
+            dst = words[:, 256 * b : 256 * b + 256, :]
             src = tp[:].rearrange("p u c -> p c u")
             if engine == "V":
                 nc.vector.tensor_copy(out=dst, in_=src)
@@ -389,12 +389,10 @@ def tile_nystroem_kernel(tc, inputs, centers, gamma, normalization, out):
             gc1 = work2.tile([P, 2048], BF16, tag="gc", align_bytes=64, name="gc")
             gx[0] = x_grouped(0)
             gx[1] = x_grouped(1)
-            tx = transpose_pair([x_sb[:, 0, :]])
-            ty = transpose_pair([x_sb[:, 1, :]])
+            tx = x_transposes(0, 0)
+            ta = c_transposes(0, 0)
             x_square(0)
             transpose_leave(tx, gx[0], 0)
-            ta = c_transposes(0, 0)
-            transpose_leave(ty, gx[0], 0, a=1)
             x_square(1)
             transpose_leave(ta, gc0, 0)
             tb = c_transposes(0, 1)
@@ -406,41 +404,44 @@ def tile_nystroem_kernel(tc, inputs, centers, gamma, normalization, out):
             x_spread_leave(0, sp)
             c_square(0, 3)
             ta = c_transposes(1, 0)
+            tb = c_transposes(1, 1)
             c_quantize(0, gc0)
             nc.vector.tensor_scalar_mul(out=g2[:], in0=g_bf[:], scalar1=2.0)
             issue1(3)
             transpose_leave(ta, gc1, 0, TC1[0])
-            tb = c_transposes(1, 1)
+            transpose_leave(tb, gc1, 1, TC1[1])
             leave1()
             issue1(4)
             leave1()
-            leave1()
-            transpose_leave(tb, gc1, 1, TC1[1])
-            leave1()
+            ta = x_transposes(1, 0)
             for t in range(4):
                 c_square(1, t)
-            ta = x_transposes(1, 0)
             c_quantize(1, gc1)
-            issue1(7)
-            dg[0] = dens_exp(0, y[0])
-            transpose_leave(ta, gx[1], 0, TX1[0])
+            issue1(5)
+            leave1()
+            issue1(6)
             tb = x_transposes(1, 1)
+            leave1()
+            issue1(7)
             for i in range(2):
+                x_square(FIRST[1] + i)
+            transpose_leave(ta, gx[1], 0, TX1[0])
+            transpose_leave(tb, gx[1], 1, TX1[1])
+            for i in range(2, 4):
                 x_square(FIRST[1] + i)
             leave1()
             issue1(8)
             leave1()
             leave1()
-            transpose_leave(tb, gx[1], 1, TX1[1])
             leave1()
-            for i in range(2, 4):
-                x_square(FIRST[1] + i)
+            dg[0] = dens_exp(0, y[0])
             x_quantize(1, gx[1])
             sp = x_spread(1)
-            dens_clip(dg[0], "V")
-            x_spread_leave(1, sp)
+            tps[0] = x_transposes(2, 0)
             issue1(10)
+            x_spread_leave(1, sp)
             norm_piece(0)
+            dens_clip(dg[0], "V")
             quantize_step(0)
 
 
@@ -455,7 +456,7 @@ def tile_nystroem_kernel(tc, inputs, centers, gamma, normalization, out):
                     issue1(len(left1) + 2)
                     if t == 0:
                         dg[s - 1] = dens_exp(steps[s - 1][0], y[s - 1])
-                        if nt and g == 0:
+                        if nt and g == 0 and s > 2:
                             tps[0] = x_transposes(q + 1, 0)
                         if nt == 4 and g == 1 and GRAM[q + 1]:
                             tps[1] = gram(gx[q + 1], range(2, 4), 0)

from contextlib import ExitStack

import concourse.mybir as mybir
from concourse.masks import make_identity

F32 = mybir.dt.float32
BF16 = mybir.dt.bfloat16
U32 = mybir.dt.uint32
U8 = mybir.dt.uint8
FP8X4 = mybir.dt.float8_e4m3fn_x4
ALU = mybir.AluOpType
ACT = mybir.ActivationFunctionType

N, D, C = 2048, 512, 1024
P = 128
FLOPS = 2 * N * D * C + 2 * N * C * C

CHUNK_TILES = [2,4,4,4,2]
FIRST = [sum(CHUNK_TILES[:q]) for q in range(len(CHUNK_TILES))]
CHUNKS = len(CHUNK_TILES)
ROOT_HALF = 0.5 ** 0.5
SLOT = {2: ["", "", "", ""], 3: ["", "", "", "S"], 4: ["", "", "S", "S"], 5: ["V", "", "SS", "S"], 6: ["V", "", "SS", "S"], 7: ["V", "", "SS", "SV"], 8: ["V", "", "SS", "SV"], 9: ["V", "", "SS", "SV"]}
NSLOT = {2: [1, 0, 1, 0], 3: [1, 0, 1, 0], 4: [0, 0, 0, 0], 5: [0, 0, 0, 0], 6: [0, 0, 0, 0], 7: [0, 0, 0, 0], 8: [0, 0, 0, 0], 9: [0, 0, 0, 0]}
NORM = "VVVV"
NORM_ORDER = [(0, 0), (1, 0), (0, 1), (1, 1)]
TAIL = ["VSVS", "VS", "VSVS"]
LAG = 2
LEAD = 2
SC = 4
SX = 4
LAST = 4
TC1 = "VV"
TX1 = "VS"
TX = "SS"
GRAM = [0,0,0,0,0]


def tile_nystroem_kernel(tc, inputs, centers, gamma, normalization, out):
    nc = tc.nc
    with ExitStack() as ctx:
        keep = ctx.enter_context(tc.tile_pool(name="keep", bufs=1))
        work2 = ctx.enter_context(tc.tile_pool(name="work2", bufs=2))
        work3 = ctx.enter_context(tc.tile_pool(name="work3", bufs=3))
        work4 = ctx.enter_context(tc.tile_pool(name="work4", bufs=4))
        junks = ctx.enter_context(tc.tile_pool(name="junks", bufs=4))
        outp = ctx.enter_context(tc.tile_pool(name="outp", bufs=6))
        ps_t = ctx.enter_context(tc.psum_pool(name="ps_t", bufs=2))
        ps_1 = ctx.enter_context(tc.psum_pool(name="ps_1", bufs=3))
        ps_2 = ctx.enter_context(tc.psum_pool(name="ps_2", bufs=3))

        x_view = inputs.rearrange("(p i) d -> p i d", i=16)
        c_view = centers.rearrange("(g p t) d -> g p t d", g=2, t=4)
        n_view = normalization.rearrange("(g p t) j -> g p t j", g=2, t=4)
        o_view = out.rearrange("(p i) j -> p i j", i=16)

        ident = keep.tile([P, P], F32)
        g_bf = keep.tile([P, 1], BF16)
        g2 = keep.tile([P, 1], F32)
        warm = keep.tile([P, 1], F32)
        c_sb = keep.tile([P, 2, 4, D], BF16)
        x_sb = keep.tile([P, 16, D], BF16)
        n_raw = keep.tile([P, 2, 4, C], BF16)
        c_codes = keep.tile([P, C], U32, align_bytes=64)
        c_scales = keep.tile([P, C], U8, align_bytes=64)
        x_codes = keep.tile([P, N], U32, align_bytes=64)
        x_scales = keep.tile([P, N], U8, align_bytes=64)
        n_codes = keep.tile([P, 2, C], U32, align_bytes=64)
        n_scales = keep.tile([P, 2, C], U8, align_bytes=64)
        x2h = keep.tile([P, 16], F32)
        c2h = keep.tile([P, 8], F32)
        x2hb = keep.tile([P, N], F32)

        nc.scalar.dma_start(out=g_bf[:], in_=gamma.partition_broadcast(P))
        nc.sync.dma_start(out=x_sb[:, 0:1, :], in_=x_view[:, 0:1, :])
        nc.sync.dma_start(out=x_sb[:, 1:2, :], in_=x_view[:, 1:2, :])
        nc.sync.dma_start(out=c_sb[:, 0, 0:2], in_=c_view[0][:, 0:2, :])
        nc.sync.dma_start(out=c_sb[:, 0, 2:4], in_=c_view[0][:, 2:4, :])
        nc.sync.dma_start(out=c_sb[:, 1], in_=c_view[1])
        nc.sync.dma_start(out=x_sb[:, 2:6, :], in_=x_view[:, 2:6, :])
        nc.sync.dma_start(out=n_raw[:, 0], in_=n_view[0])
        nc.sync.dma_start(out=n_raw[:, 1], in_=n_view[1])
        nc.sync.dma_start(out=x_sb[:, 6:10, :], in_=x_view[:, 6:10, :])
        nc.sync.dma_start(out=x_sb[:, 10:16, :], in_=x_view[:, 10:16, :])

        make_identity(nc, ident[:])
        nc.vector.memset(warm[:], 0.0)
        nc.scalar.activation(out=warm[:], in_=warm[:], func=ACT.Exp)
        def transpose_pair(rows):
            tp = ps_t.tile([P, 2, 256], F32, tag="tp", name="tp")
            for a in range(2):
                src = rows[a].bitcast(F32)
                for u in range(2):
                    nc.tensor.transpose(
                        tp[:, u, 128 * a : 128 * a + 128],
                        src[:, 128 * u : 128 * u + 128],
                        ident[:],
                    )
            return tp

        def transpose_leave(tp, grouped, b, engine="V"):
            words = grouped[:].bitcast(F32).rearrange("p (c u) -> p c u", u=2)
            dst = words[:, 256 * b : 256 * b + 256, :]
            src = tp[:].rearrange("p u c -> p c u")
            if engine == "V":
                nc.vector.tensor_copy(out=dst, in_=src)
            else:
                nc.scalar.copy(out=dst, in_=src)

        def half_square(row, col, engine="S"):
            junk = junks.tile([P, D], BF16, tag="junk" + engine, name="junk")
            if engine == "S":
                nc.scalar.activation(
                    out=junk[:], in_=row, func=ACT.Square, scale=ROOT_HALF, accum_out=col
                )
            else:
                nc.vector.scalar_tensor_tensor(
                    out=junk[:],
                    in0=row,
                    scalar=0.5,
                    in1=row,
                    op0=ALU.mult,
                    op1=ALU.mult,
                    accum_out=col,
                )

        def c_square(g, t, engine="S"):
            half_square(c_sb[:, g, t, :], c2h[:, 4 * g + t : 4 * g + t + 1], engine)

        def c_transposes(g, b):
            return transpose_pair([c_sb[:, g, 2 * b, :], c_sb[:, g, 2 * b + 1, :]])

        def gram(grouped, tiles, cols):
            rows = grouped[:].rearrange("p (n t) -> p t n", t=4)
            prod = ps_t.tile([P, len(tiles), P], F32, tag="tp", name="prod")
            for j, a in enumerate(tiles):
                for t in range(4):
                    side = rows[:, t, 128 * a : 128 * a + 128]
                    nc.tensor.matmul(
                        prod[:, j, :], lhsT=side, rhs=side, start=(t == 0), stop=(t == 3)
                    )
            return prod

        def gram_leave(prod, tiles, col_tile, first):
            for j, a in enumerate(tiles):
                junk = junks.tile([P, P], F32, tag="junkG", name="junk")
                nc.vector.scalar_tensor_tensor(
                    out=junk[:],
                    in0=prod[:, j, :],
                    scalar=0.5,
                    in1=ident[:],
                    op0=ALU.mult,
                    op1=ALU.mult,
                    accum_out=col_tile[:, first + a : first + a + 1],
                )

        def c_quantize(g, gc):
            nc.vector.quantize_mx(
                out=c_codes[:, 512 * g : 512 * g + 512].bitcast(FP8X4),
                scales=c_scales[:, 512 * g : 512 * g + 512],
                in_=gc[:],
            )

        def x_square(i):
            half_square(x_sb[:, i, :], x2h[:, i : i + 1])

        def x_grouped(q):
            return work2.tile([P, 512 * CHUNK_TILES[q]], BF16, tag="gx", align_bytes=64, name="gx")

        def x_transposes(q, b):
            i = FIRST[q] + 2 * b
            return transpose_pair([x_sb[:, i, :], x_sb[:, i + 1, :]])

        def x_quantize(q, gx):
            n0, n1 = P * FIRST[q], P * (FIRST[q] + CHUNK_TILES[q])
            nc.vector.quantize_mx(
                out=x_codes[:, n0:n1].bitcast(FP8X4), scales=x_scales[:, n0:n1], in_=gx[:]
            )

        def x_spread(q):
            nt = CHUNK_TILES[q]
            tpx = ps_t.tile([P, nt, P], F32, tag="tp", name="tpx")
            for a in range(nt):
                i = FIRST[q] + a
                nc.tensor.transpose(tpx[:, a, :], x2h[:, i : i + 1].to_broadcast([P, P]), ident[:])
            return tpx

        def x_spread_leave(q, tpx):
            nt = CHUNK_TILES[q]
            n0 = P * FIRST[q]
            nc.scalar.copy(out=x2hb[:, n0 : n0 + P * nt], in_=tpx[:].rearrange("p a c -> p (a c)"))

        def norm_group(g, half, engine):
            j0 = 512 * half
            ng = work4.tile([P, 512 * 4], BF16, tag="ng", align_bytes=64, name="ng")
            dst = ng[:].rearrange("p (c i t) -> p c t i", i=4, t=4)
            src = n_raw[:, g, :, j0 : j0 + 512].rearrange("p t (c i) -> p c t i", i=4)
            if engine == "V":
                nc.vector.tensor_copy(out=dst, in_=src)
            else:
                nc.scalar.copy(out=dst, in_=src)
            return ng

        def norm_quantize(g, half, ng):
            j0 = 512 * half
            nc.vector.quantize_mx(
                out=n_codes[:, g, j0 : j0 + 512].bitcast(FP8X4),
                scales=n_scales[:, g, j0 : j0 + 512],
                in_=ng[:],
            )

        def m1_issue(q, g, t):
            ct = 4 * g + t
            n0, n1 = P * FIRST[q], P * (FIRST[q] + CHUNK_TILES[q])
            acc = ps_1.tile([P, n1 - n0], F32, tag="acc1", name="acc1")
            nc.tensor.matmul_mx(
                out=acc[:],
                lhsT=c_codes[:, 128 * ct : 128 * ct + 128].bitcast(FP8X4),
                lhsT_scale=c_scales[:, 128 * ct : 128 * ct + 128],
                rhs=x_codes[:, n0:n1].bitcast(FP8X4),
                rhs_scale=x_scales[:, n0:n1],
                start=True,
                stop=True,
            )
            return acc

        def m1_leave(q, g, t, acc, y):
            ct = 4 * g + t
            n0, n1 = P * FIRST[q], P * (FIRST[q] + CHUNK_TILES[q])
            nc.vector.scalar_tensor_tensor(
                out=y[:, t, :],
                in0=acc[:],
                scalar=c2h[:, ct : ct + 1],
                in1=x2hb[:, n0:n1],
                op0=ALU.subtract,
                op1=ALU.subtract,
            )

        def y_tile(q):
            return work3.tile([P, 4, P * CHUNK_TILES[q]], F32, tag="y", name="y")

        def dens_exp(q, y):
            dg = work3.tile([P, 512 * CHUNK_TILES[q]], BF16, tag="dg", align_bytes=64)
            nc.scalar.activation(
                out=dg[:].rearrange("p (c i t) -> p c t i", i=4, t=4),
                in_=y[:].rearrange("p t (c i) -> p c t i", i=4),
                func=ACT.Exp,
                scale=g2[:, 0:1],
            )
            return dg

        def dens_clip(dg, engine):
            if engine == "V":
                nc.vector.tensor_scalar_min(out=dg[:], in0=dg[:], scalar1=1.0)
            else:
                nc.gpsimd.tensor_scalar(
                    out=dg[:], in0=dg[:], scalar1=1.0, scalar2=0.0, op0=ALU.min, op1=ALU.max
                )

        def dens_tiles(q):
            w = P * CHUNK_TILES[q]
            codes = work3.tile([P, 2, w], U32, tag="d_codes", align_bytes=64, name="d_codes")
            scales = work3.tile([P, 2, w], U8, tag="d_scales", align_bytes=64, name="d_scales")
            return codes, scales

        def dens_quantize(g, dg, codes, scales):
            nc.vector.quantize_mx(
                out=codes[:, g, :].bitcast(FP8X4), scales=scales[:, g, :], in_=dg[:]
            )

        o_tiles = {}

        def m2_pass(acc, q, k, g):
            codes, scales = dens[q]
            a, jh = divmod(k, 2)
            nc.tensor.matmul_mx(
                out=acc[:],
                lhsT=codes[:, g, 128 * a : 128 * a + 128].bitcast(FP8X4),
                lhsT_scale=scales[:, g, 128 * a : 128 * a + 128],
                rhs=n_codes[:, g, 512 * jh : 512 * jh + 512].bitcast(FP8X4),
                rhs_scale=n_scales[:, g, 512 * jh : 512 * jh + 512],
                start=(g == 0),
                stop=(g == 1),
            )

        def m2_issue(q, k):
            acc = ps_2.tile([P, 512], F32, tag="acc2", name="acc2")
            for g in range(2):
                m2_pass(acc, q, k, g)
            return acc

        def m2_leave(q, k, acc, engine):
            a, jh = divmod(k, 2)
            i = FIRST[q] + a
            if jh == 0:
                o_tiles[i] = outp.tile([P, C], F32, tag="o_sb", name="o_sb")
            dst = o_tiles[i][:, 512 * jh : 512 * jh + 512]
            if engine == "V":
                nc.vector.tensor_copy(out=dst, in_=acc[:])
            else:
                nc.scalar.copy(out=dst, in_=acc[:])
            if q == CHUNKS - 1:
                nc.sync.dma_start(out=o_view[:, i, 512 * jh : 512 * jh + 512], in_=dst)
            elif jh == 1:
                nc.sync.dma_start(out=o_view[:, i, :], in_=o_tiles[i][:])

        dens = {}
        y = {}
        dg = {}
        steps = [(q, g) for q in range(CHUNKS) for g in range(2)]
        slots = [(s, t) for s in range(2 * CHUNKS) for t in range(4)]
        banks = [(q, k) for q in range(CHUNKS) for k in range(2 * CHUNK_TILES[q])]
        acc1 = []
        acc2 = []
        left1 = []
        left2 = []
        done = []
        history = [0]

        def issue1(upto):
            while len(acc1) < min(upto, len(slots)):
                s, t = slots[len(acc1)]
                acc1.append(m1_issue(steps[s][0], steps[s][1], t))

        def leave1():
            s, t = slots[len(left1)]
            if t == 0:
                y[s] = y_tile(steps[s][0])
            m1_leave(steps[s][0], steps[s][1], t, acc1[len(left1)], y[s])
            left1.append(s)

        def issue2(upto):
            while len(acc2) < min(upto, len(banks) - LAST):
                q, k = banks[len(acc2)]
                acc2.append(m2_issue(q, k))

        def leave2(engines, lag):
            ready = history[max(len(history) - 1 - lag, 0)]
            for engine in engines:
                if len(left2) < min(ready, len(banks) - LAST):
                    issue2(len(left2) + 1)
                    q, k = banks[len(left2)]
                    m2_leave(q, k, acc2[len(left2)], engine)
                    left2.append(engine)
                    issue2(min(len(left2) + LEAD, ready))

        def quantize_step(s):
            q, g = steps[s]
            if g == 0:
                dens[q] = dens_tiles(q)
            dens_quantize(g, dg[s], dens[q][0], dens[q][1])
            done.append(s)

        def tick():
            n = 0
            if normed:
                for q, g in [steps[s] for s in done if steps[s][1] == 1]:
                    n += 2 * CHUNK_TILES[q]
            history.append(n)

        squares = {s: [] for s in range(2, len(steps))}
        for q in range(2, CHUNKS):
            tiles = list(range(FIRST[q], FIRST[q] + CHUNK_TILES[q]))
            if not GRAM[q]:
                early = 0 if q == 2 else len(tiles) // 2
                if early:
                    squares[2 * q - 3] = squares[2 * q - 3] + tiles[:early]
                squares[2 * q - 2] = squares[2 * q - 2] + tiles[early:]

        gx = {}
        tps = {}
        ng = {}
        normed = []

        pieces = []

        def norm_piece(k):
            if k < 4:
                gg, half = NORM_ORDER[k]
                pieces.append(norm_group(gg, half, NORM[k]))
            if 1 <= k <= 4:
                gg, half = NORM_ORDER[k - 1]
                norm_quantize(gg, half, pieces[k - 1])
            if k == 4:
                pieces.append(0)
                normed.append(0)

        def head():
            gc0 = work2.tile([P, 2048], BF16, tag="gc", align_bytes=64, name="gc")
            gc1 = work2.tile([P, 2048], BF16, tag="gc", align_bytes=64, name="gc")
            gx[0] = x_grouped(0)
            gx[1] = x_grouped(1)
            tx = x_transposes(0, 0)
            ta = c_transposes(0, 0)
            x_square(0)
            transpose_leave(tx, gx[0], 0)
            x_square(1)
            transpose_leave(ta, gc0, 0)
            tb = c_transposes(0, 1)
            sp = x_spread(0)
            x_quantize(0, gx[0])
            for t in range(3):
                c_square(0, t)
            transpose_leave(tb, gc0, 1)
            x_spread_leave(0, sp)
            c_square(0, 3)
            ta = c_transposes(1, 0)
            tb = c_transposes(1, 1)
            c_quantize(0, gc0)
            nc.vector.tensor_scalar_mul(out=g2[:], in0=g_bf[:], scalar1=2.0)
            issue1(3)
            transpose_leave(ta, gc1, 0, TC1[0])
            transpose_leave(tb, gc1, 1, TC1[1])
            leave1()
            issue1(4)
            leave1()
            ta = x_transposes(1, 0)
            for t in range(4):
                c_square(1, t)
            c_quantize(1, gc1)
            issue1(5)
            leave1()
            issue1(6)
            tb = x_transposes(1, 1)
            leave1()
            issue1(7)
            for i in range(2):
                x_square(FIRST[1] + i)
            transpose_leave(ta, gx[1], 0, TX1[0])
            transpose_leave(tb, gx[1], 1, TX1[1])
            for i in range(2, 4):
                x_square(FIRST[1] + i)
            leave1()
            issue1(8)
            leave1()
            leave1()
            leave1()
            dg[0] = dens_exp(0, y[0])
            x_quantize(1, gx[1])
            sp = x_spread(1)
            tps[0] = x_transposes(2, 0)
            issue1(10)
            x_spread_leave(1, sp)
            norm_piece(0)
            dens_clip(dg[0], "V")
            quantize_step(0)


        def run():
            for s in range(2, len(steps)):
                q, g = steps[s]
                nt = CHUNK_TILES[q + 1] if q + 1 < CHUNKS else 0
                if nt and g == 0:
                    gx[q + 1] = x_grouped(q + 1)
                for t in range(4):
                    leave1()
                    issue1(len(left1) + 2)
                    if t == 0:
                        dg[s - 1] = dens_exp(steps[s - 1][0], y[s - 1])
                        if nt and g == 0 and s > 2:
                            tps[0] = x_transposes(q + 1, 0)
                        if nt == 4 and g == 1 and GRAM[q + 1]:
                            tps[1] = gram(gx[q + 1], range(2, 4), 0)
                    if t == 1:
                        if nt and g == 0:
                            transpose_leave(tps[0], gx[q + 1], 0, TX[0])
                        if nt and g == 1:
                            x_quantize(q + 1, gx[q + 1])
                        if nt == 4 and g == 0:
                            tps[1] = x_transposes(q + 1, 1)
                        if nt and g == 0 and GRAM[q + 1]:
                            tps[0] = gram(gx[q + 1], range(0, 2), 0)
                        if nt == 4 and g == 1 and GRAM[q + 1]:
                            gram_leave(tps[1], range(2, 4), x2h, FIRST[q + 1])
                    if t == 2:
                        dens_clip(dg[s - 1], "V")
                        if nt and g == 0 and GRAM[q + 1]:
                            gram_leave(tps[0], range(0, 2), x2h, FIRST[q + 1])
                        if nt and g == 1:
                            sp = x_spread(q + 1)
                    if t in (1, 2):
                        for i in squares[s][t - 1 :: 2]:
                            x_square(i)
                    if t == 3:
                        if nt == 4 and g == 0:
                            transpose_leave(tps[1], gx[q + 1], 1, TX[1])
                        quantize_step(s - 1)
                        if nt and g == 1:
                            x_spread_leave(q + 1, sp)
                    leave2(SLOT[s][t], LAG)
                    if NSLOT[s][t]:
                        norm_piece(len(pieces))
                    tick()

            s = len(steps)
            q = CHUNKS - 1
            dg[s - 1] = dens_exp(q, y[s - 1])
            leave2(TAIL[0], 0)
            last = [
                (ps_1 if k < 3 else ps_2).tile([P, 512], F32, tag="acc1" if k < 3 else "acc2", name="last")
                for k in range(LAST)
            ]
            for k in range(2):
                m2_pass(last[k], q, k, 0)
            dens_clip(dg[s - 1], "V")
            leave2(TAIL[1], 0)
            quantize_step(s - 1)
            leave2(TAIL[2], 0)
            for k in range(LAST):
                if k >= 2:
                    m2_pass(last[k], q, k, 0)
                m2_pass(last[k], q, k, 1)
            for k in range(LAST):
                m2_leave(q, k, last[k], "SV"[k % 2])
            assert len(left2) + LAST == len(banks), len(left2)

        with tc.manual_schedule(
            engines={
                mybir.EngineType.DVE,
                mybir.EngineType.Activation,
                mybir.EngineType.PE,
            }
        ):
            head()
        run()
